import numpy as np
import ml_dtypes


def mxq(x, axis, fmt="e4m3"):
    dtype, down = {"e4m3": (ml_dtypes.float8_e4m3fn, 7), "e5m2": (ml_dtypes.float8_e5m2, 14)}[fmt]
    v = np.moveaxis(np.asarray(x, np.float32).astype(ml_dtypes.bfloat16).astype(np.float64), axis, -1)
    blocks = v.reshape(v.shape[:-1] + (-1, 32))
    amax = np.abs(blocks).max(-1, keepdims=True)
    byte = np.maximum(np.where(amax > 0, np.frexp(amax)[1] - 1 + 127, 0) - down, 1)
    scale = np.exp2(byte - 127.0)
    codes = (blocks / scale).astype(np.float32).astype(dtype).astype(np.float64)
    return np.moveaxis((codes * scale).reshape(v.shape), -1, axis)


WIDE = False


def mx_kscale(k):
    if not WIDE:
        return np.ones(k)
    levels = np.array([10, -10, 5, -5, 0])
    if k % 512:
        return np.exp2(np.random.permutation(np.resize(levels, k // 32))).repeat(32)
    a = np.empty((k // 512, 16))
    for p in range(k // 512):
        a[p, :8] = np.random.permutation(np.resize(levels, 8))
        for g in range(8):
            far = levels[np.abs(levels - a[p, g]) >= 10]
            a[p, g + 8] = far[np.random.randint(len(far))]
    return np.exp2(a.ravel()).repeat(32)


BF16 = ml_dtypes.bfloat16


def bf(x):
    return np.asarray(x, np.float32).astype(BF16)


def f64(x):
    return np.asarray(x).astype(np.float64)


B, S, D, H, DH, DR, DKV, DQ = 1, 1024, 2048, 16, 128, 64, 512, 1024
HALF = DR // 2


def rope(t, cos, sin):
    t1, t2 = t[..., 0::2], t[..., 1::2]
    c = cos[None, :, None, :]
    s = sin[None, :, None, :]
    return np.stack([t1 * c - t2 * s, t1 * s + t2 * c], axis=-1).reshape(t.shape)


def setup_inputs():
    s, t = mx_kscale(D), mx_kscale(DQ)
    ang = np.random.uniform(0.0, 2.0 * np.pi, (S, HALF))
    return {"x": bf(np.random.standard_normal((B, S, D)) * s),
            "W_q_down": bf(np.random.standard_normal((D, DQ)) / np.sqrt(D) / s[:, None] * t),
            "W_q_up": bf(np.random.standard_normal((DQ, H * DH)) / np.sqrt(DQ) / t[:, None]),
            "W_q_rope": bf(np.random.standard_normal((DQ, H * DR)) / np.sqrt(DQ) / t[:, None]),
            "rope_cos": bf(np.cos(ang)), "rope_sin": bf(np.sin(ang))}


def reference(x, W_q_down, W_q_up, W_q_rope, rope_cos, rope_sin):
    down_q = mxq(f64(x), 2, "e4m3") @ mxq(f64(W_q_down), 0, "e4m3")
    dq = mxq(down_q, 2, "e4m3")
    q_c = (dq @ mxq(f64(W_q_up), 0, "e4m3")).reshape(B, S, H, DH)
    q_r = (dq @ mxq(f64(W_q_rope), 0, "e4m3")).reshape(B, S, H, DR)
    q_r = rope(q_r, f64(rope_cos), f64(rope_sin))
    return np.concatenate([q_c, q_r], axis=-1).transpose(0, 2, 1, 3)

@@ -1,0 +1,293 @@
+from concourse import mybir
+from concourse.masks import make_identity
+
+BF16 = mybir.dt.bfloat16
+F32 = mybir.dt.float32
+U32 = mybir.dt.uint32
+U8 = mybir.dt.uint8
+FP8X4 = mybir.dt.float8_e4m3fn_x4
+MULT = mybir.AluOpType.mult
+ADD = mybir.AluOpType.add
+
+P = 128
+PACK = 4
+K_PASS = P * PACK
+BANK = 512
+
+S, D, DQ = 1024, 2048, 1024
+H, DH, DR = 16, 128, 64
+HALF = DR // 2
+J = S // P
+PAIRS = J // 2
+D_PASSES = D // K_PASS
+DQ_PASSES = DQ // K_PASS
+GROUP_HEADS = BANK // DH
+GROUPS = H // GROUP_HEADS
+ROPE_COLS = GROUP_HEADS * DR
+QUAD = 4
+
+VECTOR_COLS = 320
+
+FLOPS = 2 * S * D * DQ + 2 * S * DQ * (H * DH + H * DR)
+
+
+def tile_multiheadlatentattention_pa_kernel(
+    tc, x, w_down, w_up, w_rope, rope_cos, rope_sin, out
+):
+    nc = tc.nc
+    x_rows = x.flatten_outer_dims().rearrange("(p j) d -> p j d", j=J)
+    out_rows = out.flatten_outer_dims().rearrange("(h p j) f -> p h j f", h=H, j=J)
+
+    with tc.tile_pool(name="const", bufs=1) as const, tc.tile_pool(
+        name="raw8", bufs=6
+    ) as raw8, tc.tile_pool(name="raw4", bufs=D_PASSES) as raw4, tc.tile_pool(
+        name="wgroup", bufs=3
+    ) as wgroup, tc.tile_pool(name="agroup", bufs=2) as agroup, tc.tile_pool(
+        name="xq", bufs=J
+    ) as xq, tc.tile_pool(name="wdq", bufs=2 * D_PASSES) as wdq, tc.tile_pool(
+        name="dqq", bufs=DQ_PASSES * PAIRS
+    ) as dqq, tc.tile_pool(name="w2q", bufs=12) as w2q, tc.tile_pool(
+        name="parts", bufs=3
+    ) as parts, tc.tile_pool(name="outs", bufs=3) as outs, tc.psum_pool(
+        name="psum", bufs=8
+    ) as psum:
+        ident = const.tile([P, P], F32)
+        make_identity(nc, ident[:])
+        cos_sb = const.tile([P, J, HALF], BF16)
+        sin_sb = const.tile([P, J, HALF], BF16)
+        nc.scalar.dma_start(out=cos_sb[:], in_=rope_cos.rearrange("(p j) i -> p j i", j=J))
+        nc.scalar.dma_start(out=sin_sb[:], in_=rope_sin.rearrange("(p j) i -> p j i", j=J))
+        even_factor = const.tile([P, J, HALF, 2], F32)
+        odd_factor = const.tile([P, J, HALF, 2], F32)
+        nc.gpsimd.tensor_copy(out=even_factor[:, :, :, 0], in_=cos_sb[:])
+        nc.gpsimd.tensor_copy(out=even_factor[:, :, :, 1], in_=sin_sb[:])
+        nc.gpsimd.tensor_scalar(
+            out=odd_factor[:, :, :, 0], in0=sin_sb[:], scalar1=-1.0, scalar2=0.0, op0=MULT, op1=ADD
+        )
+        nc.gpsimd.tensor_copy(out=odd_factor[:, :, :, 1], in_=cos_sb[:])
+
+        x_raw = {}
+        wd_raw = {}
+        w2_raw = {}
+        x_codes = {}
+        wd_codes = {}
+        dq_codes = {}
+        w2_codes = {}
+
+        def load_x(pair):
+            t = raw8.tile([P, 2 * D], BF16, tag="raw8", name="x_raw")
+            nc.sync.dma_start(
+                out=t[:].rearrange("p (j d) -> p j d", j=2), in_=x_rows[:, 2 * pair : 2 * pair + 2, :]
+            )
+            x_raw[pair] = t
+
+        def load_w_down(half):
+            cols = slice(half * BANK, (half + 1) * BANK)
+            for c in range(D_PASSES):
+                t = raw4.tile([P, PACK, BANK], BF16, tag="raw4", name="wd_raw")
+                nc.sync.dma_start(
+                    out=t[:],
+                    in_=w_down[c * K_PASS : (c + 1) * K_PASS, cols].rearrange("(p t) n -> p t n", t=PACK),
+                )
+                wd_raw[(c, half)] = t
+
+        def load_stage2(key):
+            name, g, half = key
+            src = w_up[:, half * 2 * BANK : (half + 1) * 2 * BANK] if name == "up" else w_rope
+            t = raw8.tile([P, PACK, 2 * BANK], BF16, tag="raw8", name="w2_raw")
+            nc.sync.dma_start(
+                out=t[:], in_=src[g * K_PASS : (g + 1) * K_PASS, :].rearrange("(p t) n -> p t n", t=PACK)
+            )
+            w2_raw[key] = t
+
+        stage2_order = []
+        for half in range(2):
+            for g in range(DQ_PASSES):
+                stage2_order.append(("up", g, half))
+            if half == 0:
+                for g in range(DQ_PASSES):
+                    stage2_order.append(("rope", g, 0))
+
+        def quantise_weight_block(pool, rows, permute):
+            grouped = wgroup.tile([P, BANK, PACK], BF16, align_bytes=64, tag="wg", name="grouped")
+            cols = "(i c)" if permute else "(c i)"
+            dst = grouped[:].rearrange("p %s t -> p c t i" % cols, i=4)
+            src = rows.rearrange("p t (c i) -> p c t i", i=4)
+            v = VECTOR_COLS // 4
+            nc.vector.tensor_copy(out=dst[:, 0:v, :, :], in_=src[:, 0:v, :, :])
+            nc.scalar.copy(out=dst[:, v : BANK // 4, :, :], in_=src[:, v : BANK // 4, :, :])
+            codes = pool.tile([P, BANK], U32, align_bytes=64, tag="codes", name="codes")
+            scales = pool.tile([P, BANK], U8, align_bytes=64, tag="scales", name="scales")
+            nc.vector.quantize_mx(
+                out=codes[:].bitcast(FP8X4),
+                scales=scales[:],
+                in_=grouped[:].rearrange("p n t -> p (n t)"),
+            )
+            return codes, scales
+
+        def x_to_codes(pair):
+            words = x_raw[pair][:].bitcast(F32)
+            for jl in range(2):
+                grouped = agroup.tile([P, D], BF16, align_bytes=64, tag="xg", name="x_grouped")
+                grouped_words = grouped[:].bitcast(F32).rearrange(
+                    "q (c s u) -> q c s u", c=D_PASSES, u=2
+                )
+                for b in range(2):
+                    xt = psum.tile([P, BANK], F32, tag="bank", name="xt")
+                    for cl in range(2):
+                        for u in range(2):
+                            col0 = jl * (D // 2) + (2 * b + cl) * 2 * P
+                            nc.tensor.transpose(
+                                xt[:, (2 * cl + u) * P : (2 * cl + u + 1) * P],
+                                words[:, col0 + u : col0 + 2 * P : 2],
+                                ident[:],
+                            )
+                    nc.scalar.copy(
+                        out=grouped_words[:, 2 * b : 2 * b + 2, :, :],
+                        in_=xt[:].rearrange("q (c u s) -> q c s u", c=2, u=2),
+                    )
+                codes = xq.tile([P, D_PASSES * P], U32, align_bytes=64, tag="codes", name="x_codes")
+                scales = xq.tile([P, D_PASSES * P], U8, align_bytes=64, tag="scales", name="x_scales")
+                nc.vector.quantize_mx(out=codes[:].bitcast(FP8X4), scales=scales[:], in_=grouped[:])
+                x_codes[2 * pair + jl] = (codes, scales)
+
+        def down_projection(half, pair):
+            grouped = agroup.tile([P, 2, P, PACK], BF16, align_bytes=64, tag="dqg", name="dq_grouped")
+            for jl in range(2):
+                xc, xs = x_codes[2 * pair + jl]
+                acc = psum.tile([P, BANK], F32, tag="bank", name="dq_acc")
+                for t in range(PACK):
+                    for c in range(D_PASSES):
+                        wc, ws = wd_codes[(c, half)]
+                        nc.tensor.matmul_mx(
+                            out=acc[:, t * P : (t + 1) * P],
+                            lhsT=wc[:, t * P : (t + 1) * P].bitcast(FP8X4),
+                            lhsT_scale=ws[:, t * P : (t + 1) * P],
+                            rhs=xc[:, c * P : (c + 1) * P].bitcast(FP8X4),
+                            rhs_scale=xs[:, c * P : (c + 1) * P],
+                            start=(c == 0),
+                            stop=(c == D_PASSES - 1),
+                        )
+                nc.scalar.copy(
+                    out=grouped[:, jl, :, :], in_=acc[:].rearrange("p (t s) -> p s t", t=PACK)
+                )
+            codes = dqq.tile([P, 2 * P], U32, align_bytes=64, tag="codes", name="dq_codes")
+            scales = dqq.tile([P, 2 * P], U8, align_bytes=64, tag="scales", name="dq_scales")
+            nc.vector.quantize_mx(
+                out=codes[:].bitcast(FP8X4),
+                scales=scales[:],
+                in_=grouped[:].rearrange("p j s t -> p (j s t)"),
+            )
+            dq_codes[(half, pair)] = (codes, scales)
+
+        stage2_blocks = []
+        for group in range(GROUPS):
+            for g in range(DQ_PASSES):
+                stage2_blocks.append(("up", g, group))
+            if group % 2 == 0:
+                for g in range(DQ_PASSES):
+                    stage2_blocks.append(("rope", g, group // 2))
+
+        def quantise_stage2_block(n):
+            name, g, part = stage2_blocks[n]
+            rows = w2_raw[("up", g, part // 2)] if name == "up" else w2_raw[("rope", g, 0)]
+            side = part % 2
+            w2_codes[stage2_blocks[n]] = quantise_weight_block(
+                w2q, rows[:, :, side * BANK : (side + 1) * BANK], False
+            )
+
+        def up_projection(acc, j, weights, col0, width):
+            for g in range(DQ_PASSES):
+                ac, asc = dq_codes[(g, j // 2)]
+                wc, ws = weights[g]
+                tok = slice((j % 2) * P, (j % 2 + 1) * P)
+                nc.tensor.matmul_mx(
+                    out=acc,
+                    lhsT=ac[:, tok].bitcast(FP8X4),
+                    lhsT_scale=asc[:, tok],
+                    rhs=wc[:, col0 : col0 + width].bitcast(FP8X4),
+                    rhs_scale=ws[:, col0 : col0 + width],
+                    start=(g == 0),
+                    stop=(g == DQ_PASSES - 1),
+                )
+
+        def head_group(group):
+            up_w = [w2_codes[("up", g, group)] for g in range(DQ_PASSES)]
+            rope_w = [w2_codes[("rope", g, group // 2)] for g in range(DQ_PASSES)]
+            shape = [P, 2, GROUP_HEADS, HALF, 2]
+            heads = slice(group * GROUP_HEADS, (group + 1) * GROUP_HEADS)
+            for quad in range(J // QUAD):
+                result = outs.tile([P, GROUP_HEADS, QUAD, DH + DR], F32, tag="res", name="result")
+                for jp in range(QUAD // 2):
+                    j0 = quad * QUAD + 2 * jp
+                    qr = psum.tile([P, BANK], F32, tag="bank", name="qr")
+                    for jl in range(2):
+                        up_projection(
+                            qr[:, jl * ROPE_COLS : (jl + 1) * ROPE_COLS],
+                            j0 + jl,
+                            rope_w,
+                            (group % 2) * ROPE_COLS,
+                            ROPE_COLS,
+                        )
+                    pairs = qr[:].rearrange("p (j h i e) -> p j h i e", j=2, h=GROUP_HEADS, e=2)
+                    even_part = parts.tile(shape, F32, tag="even", name="even_part")
+                    odd_part = parts.tile(shape, F32, tag="odd", name="odd_part")
+                    nc.vector.tensor_tensor(
+                        out=even_part[:],
+                        in0=pairs[:, :, :, :, 0:1].to_broadcast(shape),
+                        in1=even_factor[:, j0 : j0 + 2, :, :].unsqueeze(2).to_broadcast(shape),
+                        op=MULT,
+                    )
+                    nc.vector.tensor_tensor(
+                        out=odd_part[:],
+                        in0=pairs[:, :, :, :, 1:2].to_broadcast(shape),
+                        in1=odd_factor[:, j0 : j0 + 2, :, :].unsqueeze(2).to_broadcast(shape),
+                        op=MULT,
+                    )
+                    nc.gpsimd.tensor_tensor(
+                        out=result[:, :, 2 * jp : 2 * jp + 2, DH : DH + DR],
+                        in0=even_part[:].rearrange("p j h i e -> p h j (i e)"),
+                        in1=odd_part[:].rearrange("p j h i e -> p h j (i e)"),
+                        op=ADD,
+                    )
+                n_quad = group * (J // QUAD) + quad
+                pieces = 2 if n_quad == 0 or n_quad == GROUPS * (J // QUAD) - 1 else 1
+                width = QUAD // pieces
+                for jj in range(QUAD):
+                    qc = psum.tile([P, BANK], F32, tag="bank", name="qc")
+                    up_projection(qc[:], quad * QUAD + jj, up_w, 0, BANK)
+                    nc.scalar.copy(
+                        out=result[:, :, jj, 0:DH],
+                        in_=qc[:].rearrange("p (h d) -> p h d", h=GROUP_HEADS),
+                    )
+                    if jj % 2 == 1:
+                        step = PAIRS + 2 * n_quad + jj // 2
+                        if step < len(stage2_blocks):
+                            quantise_stage2_block(step)
+                    if (jj + 1) % width == 0:
+                        nc.sync.dma_start(
+                            out=out_rows[:, heads, quad * QUAD + jj + 1 - width : quad * QUAD + jj + 1, :],
+                            in_=result[:, :, jj + 1 - width : jj + 1, :],
+                        )
+
+        load_x(0)
+        load_w_down(0)
+        for pair in range(1, PAIRS):
+            load_x(pair)
+        x_to_codes(0)
+        for c in range(D_PASSES):
+            wd_codes[(c, 0)] = quantise_weight_block(wdq, wd_raw[(c, 0)][:], True)
+        load_w_down(1)
+        for n in range(3):
+            load_stage2(stage2_order[n])
+        for pair in range(PAIRS):
+            if pair + 1 < PAIRS:
+                x_to_codes(pair + 1)
+                load_stage2(stage2_order[pair + 3])
+            down_projection(0, pair)
+            wd_codes[(pair, 1)] = quantise_weight_block(wdq, wd_raw[(pair, 1)][:], True)
+        for pair in range(PAIRS):
+            down_projection(1, pair)
+            quantise_stage2_block(pair)
+        for group in range(GROUPS):
+            head_group(group)

@@ -18,7 +18,6 @@ S, D, DQ = 1024, 2048, 1024
 H, DH, DR = 16, 128, 64
 HALF = DR // 2
 J = S // P
-PAIRS = J // 2
 D_PASSES = D // K_PASS
 DQ_PASSES = DQ // K_PASS
 GROUP_HEADS = BANK // DH
@@ -39,162 +38,143 @@ def tile_multiheadlatentattention_pa_kernel(
     out_rows = out.flatten_outer_dims().rearrange("(h p j) f -> p h j f", h=H, j=J)
 
     with tc.tile_pool(name="const", bufs=1) as const, tc.tile_pool(
-        name="raw8", bufs=6
-    ) as raw8, tc.tile_pool(name="raw4", bufs=D_PASSES) as raw4, tc.tile_pool(
-        name="wgroup", bufs=3
-    ) as wgroup, tc.tile_pool(name="agroup", bufs=2) as agroup, tc.tile_pool(
-        name="xq", bufs=J
-    ) as xq, tc.tile_pool(name="wdq", bufs=2 * D_PASSES) as wdq, tc.tile_pool(
-        name="dqq", bufs=DQ_PASSES * PAIRS
-    ) as dqq, tc.tile_pool(name="w2q", bufs=12) as w2q, tc.tile_pool(
-        name="parts", bufs=3
-    ) as parts, tc.tile_pool(name="outs", bufs=3) as outs, tc.psum_pool(
-        name="psum", bufs=8
-    ) as psum:
-        ident = const.tile([P, P], F32)
-        make_identity(nc, ident[:])
-        cos_sb = const.tile([P, J, HALF], BF16)
-        sin_sb = const.tile([P, J, HALF], BF16)
-        nc.scalar.dma_start(out=cos_sb[:], in_=rope_cos.rearrange("(p j) i -> p j i", j=J))
-        nc.scalar.dma_start(out=sin_sb[:], in_=rope_sin.rearrange("(p j) i -> p j i", j=J))
-        even_factor = const.tile([P, J, HALF, 2], F32)
-        odd_factor = const.tile([P, J, HALF, 2], F32)
-        nc.gpsimd.tensor_copy(out=even_factor[:, :, :, 0], in_=cos_sb[:])
-        nc.gpsimd.tensor_copy(out=even_factor[:, :, :, 1], in_=sin_sb[:])
-        nc.gpsimd.tensor_scalar(
-            out=odd_factor[:, :, :, 0], in0=sin_sb[:], scalar1=-1.0, scalar2=0.0, op0=MULT, op1=ADD
-        )
-        nc.gpsimd.tensor_copy(out=odd_factor[:, :, :, 1], in_=cos_sb[:])
+        name="xraw", bufs=4
+    ) as xraw, tc.tile_pool(name="wdraw", bufs=6) as wdraw, tc.tile_pool(
+        name="w2raw", bufs=5
+    ) as w2raw, tc.tile_pool(name="wgroup", bufs=3) as wgroup, tc.tile_pool(
+        name="agroup", bufs=2
+    ) as agroup, tc.tile_pool(name="xq", bufs=6) as xq, tc.tile_pool(
+        name="wdq", bufs=2 * D_PASSES
+    ) as wdq, tc.tile_pool(name="dqq", bufs=J) as dqq, tc.tile_pool(
+        name="w2q", bufs=12
+    ) as w2q, tc.tile_pool(name="parts", bufs=2) as parts, tc.tile_pool(
+        name="outs", bufs=3
+    ) as outs, tc.psum_pool(name="psum", bufs=8) as psum, tc.manual_schedule():
+        x_raw, wd_raw, w2_raw = {}, {}, {}
+        x_grouped, x_codes = {}, {}
+        grouped_blocks, w_codes = {}, {}
+        dq_acc, dq_grouped, dq_codes = {}, {}, {}
+        xt_banks = {}
+        results = {}
 
-        x_raw = {}
-        wd_raw = {}
-        w2_raw = {}
-        x_codes = {}
-        wd_codes = {}
-        dq_codes = {}
-        w2_codes = {}
+        def load_x(j):
+            t = xraw.tile([P, D], BF16, tag="x", name="x_raw")
+            nc.sync.dma_start(out=t[:], in_=x_rows[:, j, :])
+            x_raw[j] = t
 
-        def load_x(pair):
-            t = raw8.tile([P, 2 * D], BF16, tag="raw8", name="x_raw")
+        def load_w_down(half, c):
+            t = wdraw.tile([P, PACK, BANK], BF16, tag="wd", name="wd_raw")
             nc.sync.dma_start(
-                out=t[:].rearrange("p (j d) -> p j d", j=2), in_=x_rows[:, 2 * pair : 2 * pair + 2, :]
+                out=t[:],
+                in_=w_down[c * K_PASS : (c + 1) * K_PASS, half * BANK : (half + 1) * BANK].rearrange(
+                    "(p t) n -> p t n", t=PACK
+                ),
             )
-            x_raw[pair] = t
+            wd_raw[("down", c, half)] = t
 
-        def load_w_down(half):
-            cols = slice(half * BANK, (half + 1) * BANK)
-            for c in range(D_PASSES):
-                t = raw4.tile([P, PACK, BANK], BF16, tag="raw4", name="wd_raw")
-                nc.sync.dma_start(
-                    out=t[:],
-                    in_=w_down[c * K_PASS : (c + 1) * K_PASS, cols].rearrange("(p t) n -> p t n", t=PACK),
-                )
-                wd_raw[(c, half)] = t
-
-        def load_stage2(key):
-            name, g, half = key
+        def load_stage2(name, g, half):
             src = w_up[:, half * 2 * BANK : (half + 1) * 2 * BANK] if name == "up" else w_rope
-            t = raw8.tile([P, PACK, 2 * BANK], BF16, tag="raw8", name="w2_raw")
+            t = w2raw.tile([P, PACK, 2 * BANK], BF16, tag="w2", name="w2_raw")
             nc.sync.dma_start(
                 out=t[:], in_=src[g * K_PASS : (g + 1) * K_PASS, :].rearrange("(p t) n -> p t n", t=PACK)
             )
-            w2_raw[key] = t
+            w2_raw[(name, g, half)] = t
 
-        stage2_order = []
-        for half in range(2):
-            for g in range(DQ_PASSES):
-                stage2_order.append(("up", g, half))
-            if half == 0:
-                for g in range(DQ_PASSES):
-                    stage2_order.append(("rope", g, 0))
-
-        def quantise_weight_block(pool, rows, permute):
+        def regroup(key):
+            name, g, part = key
+            if name == "down":
+                rows = wd_raw[key][:]
+            else:
+                raw = w2_raw[(name, g, part // 2 if name == "up" else 0)]
+                rows = raw[:, :, (part % 2) * BANK : (part % 2 + 1) * BANK]
             grouped = wgroup.tile([P, BANK, PACK], BF16, align_bytes=64, tag="wg", name="grouped")
-            cols = "(i c)" if permute else "(c i)"
+            cols = "(i c)" if name == "down" else "(c i)"
             dst = grouped[:].rearrange("p %s t -> p c t i" % cols, i=4)
             src = rows.rearrange("p t (c i) -> p c t i", i=4)
             v = VECTOR_COLS // 4
             nc.vector.tensor_copy(out=dst[:, 0:v, :, :], in_=src[:, 0:v, :, :])
             nc.scalar.copy(out=dst[:, v : BANK // 4, :, :], in_=src[:, v : BANK // 4, :, :])
-            codes = pool.tile([P, BANK], U32, align_bytes=64, tag="codes", name="codes")
-            scales = pool.tile([P, BANK], U8, align_bytes=64, tag="scales", name="scales")
+            grouped_blocks[key] = grouped
+
+        def quantise(key):
+            pool = wdq if key[0] == "down" else w2q
+            codes = pool.tile([P, BANK], U32, align_bytes=64, tag="codes", name="w_codes")
+            scales = pool.tile([P, BANK], U8, align_bytes=64, tag="scales", name="w_scales")
             nc.vector.quantize_mx(
                 out=codes[:].bitcast(FP8X4),
                 scales=scales[:],
-                in_=grouped[:].rearrange("p n t -> p (n t)"),
+                in_=grouped_blocks[key][:].rearrange("p n t -> p (n t)"),
             )
-            return codes, scales
+            w_codes[key] = (codes, scales)
 
-        def x_to_codes(pair):
-            words = x_raw[pair][:].bitcast(F32)
-            for jl in range(2):
-                grouped = agroup.tile([P, D], BF16, align_bytes=64, tag="xg", name="x_grouped")
-                grouped_words = grouped[:].bitcast(F32).rearrange(
-                    "q (c s u) -> q c s u", c=D_PASSES, u=2
-                )
-                for b in range(2):
-                    xt = psum.tile([P, BANK], F32, tag="bank", name="xt")
-                    for cl in range(2):
-                        for u in range(2):
-                            col0 = jl * (D // 2) + (2 * b + cl) * 2 * P
-                            nc.tensor.transpose(
-                                xt[:, (2 * cl + u) * P : (2 * cl + u + 1) * P],
-                                words[:, col0 + u : col0 + 2 * P : 2],
-                                ident[:],
-                            )
-                    nc.scalar.copy(
-                        out=grouped_words[:, 2 * b : 2 * b + 2, :, :],
-                        in_=xt[:].rearrange("q (c u s) -> q c s u", c=2, u=2),
-                    )
-                codes = xq.tile([P, D_PASSES * P], U32, align_bytes=64, tag="codes", name="x_codes")
-                scales = xq.tile([P, D_PASSES * P], U8, align_bytes=64, tag="scales", name="x_scales")
-                nc.vector.quantize_mx(out=codes[:].bitcast(FP8X4), scales=scales[:], in_=grouped[:])
-                x_codes[2 * pair + jl] = (codes, scales)
-
-        def down_projection(half, pair):
-            grouped = agroup.tile([P, 2, P, PACK], BF16, align_bytes=64, tag="dqg", name="dq_grouped")
-            for jl in range(2):
-                xc, xs = x_codes[2 * pair + jl]
-                acc = psum.tile([P, BANK], F32, tag="bank", name="dq_acc")
-                for t in range(PACK):
-                    for c in range(D_PASSES):
-                        wc, ws = wd_codes[(c, half)]
-                        nc.tensor.matmul_mx(
-                            out=acc[:, t * P : (t + 1) * P],
-                            lhsT=wc[:, t * P : (t + 1) * P].bitcast(FP8X4),
-                            lhsT_scale=ws[:, t * P : (t + 1) * P],
-                            rhs=xc[:, c * P : (c + 1) * P].bitcast(FP8X4),
-                            rhs_scale=xs[:, c * P : (c + 1) * P],
-                            start=(c == 0),
-                            stop=(c == D_PASSES - 1),
+        def transpose_x(j):
+            words = x_raw[j][:].bitcast(F32)
+            banks = []
+            for b in range(2):
+                xt = psum.tile([P, BANK], F32, tag="bank", name="xt")
+                for cl in range(2):
+                    for u in range(2):
+                        col0 = (2 * b + cl) * 2 * P
+                        nc.tensor.transpose(
+                            xt[:, (2 * cl + u) * P : (2 * cl + u + 1) * P],
+                            words[:, col0 + u : col0 + 2 * P : 2],
+                            ident[:],
                         )
+                banks.append(xt)
+            xt_banks[j] = banks
+
+        def copy_x(j):
+            grouped = agroup.tile([P, D], BF16, align_bytes=64, tag="xg", name="x_grouped")
+            words = grouped[:].bitcast(F32).rearrange("q (c s u) -> q c s u", c=D_PASSES, u=2)
+            for b in range(2):
                 nc.scalar.copy(
-                    out=grouped[:, jl, :, :], in_=acc[:].rearrange("p (t s) -> p s t", t=PACK)
+                    out=words[:, 2 * b : 2 * b + 2, :, :],
+                    in_=xt_banks[j][b][:].rearrange("q (c u s) -> q c s u", c=2, u=2),
                 )
+            x_grouped[j] = grouped
+
+        def quantise_x(j):
+            codes = xq.tile([P, D_PASSES * P], U32, align_bytes=64, tag="codes", name="x_codes")
+            scales = xq.tile([P, D_PASSES * P], U8, align_bytes=64, tag="scales", name="x_scales")
+            nc.vector.quantize_mx(out=codes[:].bitcast(FP8X4), scales=scales[:], in_=x_grouped[j][:])
+            x_codes[j] = (codes, scales)
+
+        def down_projection(half, j):
+            xc, xs = x_codes[j]
+            acc = psum.tile([P, BANK], F32, tag="bank", name="dq_acc")
+            for t in range(PACK):
+                for c in range(D_PASSES):
+                    wc, ws = w_codes[("down", c, half)]
+                    nc.tensor.matmul_mx(
+                        out=acc[:, t * P : (t + 1) * P],
+                        lhsT=wc[:, t * P : (t + 1) * P].bitcast(FP8X4),
+                        lhsT_scale=ws[:, t * P : (t + 1) * P],
+                        rhs=xc[:, c * P : (c + 1) * P].bitcast(FP8X4),
+                        rhs_scale=xs[:, c * P : (c + 1) * P],
+                        start=(c == 0),
+                        stop=(c == D_PASSES - 1),
+                    )
+            dq_acc[(half, j)] = acc
+
+        def copy_dq(half, j):
+            if j % 2 == 0:
+                dq_grouped[(half, j // 2)] = agroup.tile(
+                    [P, 2, P, PACK], BF16, align_bytes=64, tag="dqg", name="dq_grouped"
+                )
+            nc.scalar.copy(
+                out=dq_grouped[(half, j // 2)][:, j % 2, :, :],
+                in_=dq_acc[(half, j)][:].rearrange("p (t s) -> p s t", t=PACK),
+            )
+
+        def quantise_dq(half, pair):
             codes = dqq.tile([P, 2 * P], U32, align_bytes=64, tag="codes", name="dq_codes")
             scales = dqq.tile([P, 2 * P], U8, align_bytes=64, tag="scales", name="dq_scales")
             nc.vector.quantize_mx(
                 out=codes[:].bitcast(FP8X4),
                 scales=scales[:],
-                in_=grouped[:].rearrange("p j s t -> p (j s t)"),
+                in_=dq_grouped[(half, pair)][:].rearrange("p j s t -> p (j s t)"),
             )
             dq_codes[(half, pair)] = (codes, scales)
-
-        stage2_blocks = []
-        for group in range(GROUPS):
-            for g in range(DQ_PASSES):
-                stage2_blocks.append(("up", g, group))
-            if group % 2 == 0:
-                for g in range(DQ_PASSES):
-                    stage2_blocks.append(("rope", g, group // 2))
-
-        def quantise_stage2_block(n):
-            name, g, part = stage2_blocks[n]
-            rows = w2_raw[("up", g, part // 2)] if name == "up" else w2_raw[("rope", g, 0)]
-            side = part % 2
-            w2_codes[stage2_blocks[n]] = quantise_weight_block(
-                w2q, rows[:, :, side * BANK : (side + 1) * BANK], False
-            )
 
         def up_projection(acc, j, weights, col0, width):
             for g in range(DQ_PASSES):
@@ -211,83 +191,185 @@ def tile_multiheadlatentattention_pa_kernel(
                     stop=(g == DQ_PASSES - 1),
                 )
 
-        def head_group(group):
-            up_w = [w2_codes[("up", g, group)] for g in range(DQ_PASSES)]
-            rope_w = [w2_codes[("rope", g, group // 2)] for g in range(DQ_PASSES)]
-            shape = [P, 2, GROUP_HEADS, HALF, 2]
-            heads = slice(group * GROUP_HEADS, (group + 1) * GROUP_HEADS)
-            for quad in range(J // QUAD):
-                result = outs.tile([P, GROUP_HEADS, QUAD, DH + DR], F32, tag="res", name="result")
-                for jp in range(QUAD // 2):
-                    j0 = quad * QUAD + 2 * jp
-                    qr = psum.tile([P, BANK], F32, tag="bank", name="qr")
-                    for jl in range(2):
-                        up_projection(
-                            qr[:, jl * ROPE_COLS : (jl + 1) * ROPE_COLS],
-                            j0 + jl,
-                            rope_w,
-                            (group % 2) * ROPE_COLS,
-                            ROPE_COLS,
-                        )
-                    pairs = qr[:].rearrange("p (j h i e) -> p j h i e", j=2, h=GROUP_HEADS, e=2)
-                    even_part = parts.tile(shape, F32, tag="even", name="even_part")
-                    odd_part = parts.tile(shape, F32, tag="odd", name="odd_part")
-                    nc.vector.tensor_tensor(
-                        out=even_part[:],
-                        in0=pairs[:, :, :, :, 0:1].to_broadcast(shape),
-                        in1=even_factor[:, j0 : j0 + 2, :, :].unsqueeze(2).to_broadcast(shape),
-                        op=MULT,
-                    )
-                    nc.vector.tensor_tensor(
-                        out=odd_part[:],
-                        in0=pairs[:, :, :, :, 1:2].to_broadcast(shape),
-                        in1=odd_factor[:, j0 : j0 + 2, :, :].unsqueeze(2).to_broadcast(shape),
-                        op=MULT,
-                    )
-                    nc.gpsimd.tensor_tensor(
-                        out=result[:, :, 2 * jp : 2 * jp + 2, DH : DH + DR],
-                        in0=even_part[:].rearrange("p j h i e -> p h j (i e)"),
-                        in1=odd_part[:].rearrange("p j h i e -> p h j (i e)"),
-                        op=ADD,
-                    )
-                n_quad = group * (J // QUAD) + quad
-                pieces = 2 if n_quad == 0 or n_quad == GROUPS * (J // QUAD) - 1 else 1
-                width = QUAD // pieces
-                for jj in range(QUAD):
-                    qc = psum.tile([P, BANK], F32, tag="bank", name="qc")
-                    up_projection(qc[:], quad * QUAD + jj, up_w, 0, BANK)
-                    nc.scalar.copy(
-                        out=result[:, :, jj, 0:DH],
-                        in_=qc[:].rearrange("p (h d) -> p h d", h=GROUP_HEADS),
-                    )
-                    if jj % 2 == 1:
-                        step = PAIRS + 2 * n_quad + jj // 2
-                        if step < len(stage2_blocks):
-                            quantise_stage2_block(step)
-                    if (jj + 1) % width == 0:
-                        nc.sync.dma_start(
-                            out=out_rows[:, heads, quad * QUAD + jj + 1 - width : quad * QUAD + jj + 1, :],
-                            in_=result[:, :, jj + 1 - width : jj + 1, :],
-                        )
+        def rotary(group, quad, jp):
+            if jp == 0:
+                results[(group, quad)] = outs.tile(
+                    [P, GROUP_HEADS, QUAD, DH + DR], F32, tag="res", name="result"
+                )
+            result = results[(group, quad)]
+            rope_w = [w_codes[("rope", g, group // 2)] for g in range(DQ_PASSES)]
+            j0 = quad * QUAD + 2 * jp
+            qr = psum.tile([P, BANK], F32, tag="bank", name="qr")
+            for jl in range(2):
+                up_projection(
+                    qr[:, jl * ROPE_COLS : (jl + 1) * ROPE_COLS],
+                    j0 + jl,
+                    rope_w,
+                    (group % 2) * ROPE_COLS,
+                    ROPE_COLS,
+                )
+            shape = [P, 2, GROUP_HEADS, HALF, 2, 2]
+            products = parts.tile(shape, F32, tag="prod", name="products")
+            nc.vector.tensor_tensor(
+                out=products[:],
+                in0=qr[:]
+                .rearrange("p (j h i a) -> p j h i a", j=2, h=GROUP_HEADS, a=2)
+                .unsqueeze(4)
+                .to_broadcast(shape),
+                in1=factor[:, j0 : j0 + 2, :, :, :].unsqueeze(2).to_broadcast(shape),
+                op=MULT,
+            )
+            nc.gpsimd.tensor_tensor(
+                out=result[:, :, 2 * jp : 2 * jp + 2, DH : DH + DR],
+                in0=products[:, :, :, :, :, 0].rearrange("p j h i e -> p h j (i e)"),
+                in1=products[:, :, :, :, :, 1].rearrange("p j h i e -> p h j (i e)"),
+                op=ADD,
+            )
 
+        def content(group, quad, jj):
+            up_w = [w_codes[("up", g, group)] for g in range(DQ_PASSES)]
+            qc = psum.tile([P, BANK], F32, tag="bank", name="qc")
+            up_projection(qc[:], quad * QUAD + jj, up_w, 0, BANK)
+            nc.scalar.copy(
+                out=results[(group, quad)][:, :, jj, 0:DH],
+                in_=qc[:].rearrange("p (h d) -> p h d", h=GROUP_HEADS),
+            )
+
+        def store(group, quad, first, last):
+            heads = slice(group * GROUP_HEADS, (group + 1) * GROUP_HEADS)
+            nc.sync.dma_start(
+                out=out_rows[:, heads, quad * QUAD + first : quad * QUAD + last, :],
+                in_=results[(group, quad)][:, :, first:last, :],
+            )
+
+        load_w_down(0, 0)
         load_x(0)
-        load_w_down(0)
-        for pair in range(1, PAIRS):
-            load_x(pair)
-        x_to_codes(0)
+        ident = const.tile([P, P], F32)
+        make_identity(nc, ident[:])
+        cos_sb = const.tile([P, J, HALF], BF16)
+        sin_sb = const.tile([P, J, HALF], BF16)
+        nc.scalar.dma_start(out=cos_sb[:], in_=rope_cos.rearrange("(p j) i -> p j i", j=J))
+        nc.scalar.dma_start(out=sin_sb[:], in_=rope_sin.rearrange("(p j) i -> p j i", j=J))
+        factor = const.tile([P, J, HALF, 2, 2], F32)
+        nc.gpsimd.tensor_copy(out=factor[:, :, :, 0, 0], in_=cos_sb[:])
+        nc.gpsimd.tensor_copy(out=factor[:, :, :, 1, 0], in_=sin_sb[:])
+        nc.gpsimd.tensor_scalar(
+            out=factor[:, :, :, 0, 1], in0=sin_sb[:], scalar1=-1.0, scalar2=0.0, op0=MULT, op1=ADD
+        )
+        nc.gpsimd.tensor_copy(out=factor[:, :, :, 1, 1], in_=cos_sb[:])
+
+        for c in range(1, D_PASSES):
+            load_w_down(0, c)
+            load_x(c)
+        for c in range(2):
+            load_w_down(1, c)
+
         for c in range(D_PASSES):
-            wd_codes[(c, 0)] = quantise_weight_block(wdq, wd_raw[(c, 0)][:], True)
-        load_w_down(1)
-        for n in range(3):
-            load_stage2(stage2_order[n])
-        for pair in range(PAIRS):
-            if pair + 1 < PAIRS:
-                x_to_codes(pair + 1)
-                load_stage2(stage2_order[pair + 3])
-            down_projection(0, pair)
-            wd_codes[(pair, 1)] = quantise_weight_block(wdq, wd_raw[(pair, 1)][:], True)
-        for pair in range(PAIRS):
-            down_projection(1, pair)
-            quantise_stage2_block(pair)
-        for group in range(GROUPS):
-            head_group(group)
+            transpose_x(c)
+            regroup(("down", c, 0))
+            copy_x(c)
+            if c > 0:
+                quantise(("down", c - 1, 0))
+                quantise_x(c - 1)
+        for c in range(2, D_PASSES):
+            load_w_down(1, c)
+        load_stage2("up", 0, 0)
+        load_stage2("up", 1, 0)
+        load_x(4)
+        load_x(5)
+        load_stage2("rope", 0, 0)
+        load_stage2("rope", 1, 0)
+        load_x(6)
+        load_x(7)
+        load_stage2("up", 0, 1)
+
+        regroup(("down", 0, 1))
+        quantise(("down", D_PASSES - 1, 0))
+        quantise_x(D_PASSES - 1)
+        for c in range(D_PASSES):
+            down_projection(0, c)
+            if c > 0:
+                regroup(("down", c, 1))
+            copy_dq(0, c)
+            if c > 0:
+                quantise(("down", c - 1, 1))
+            if c == 2:
+                quantise_dq(0, 0)
+
+        first_blocks = [("up", 0, 0), ("up", 1, 0), ("rope", 0, 0), ("rope", 1, 0)]
+        regroup(first_blocks[0])
+        quantise(("down", D_PASSES - 1, 1))
+        quantise_dq(0, 1)
+        for c in range(4):
+            down_projection(1, c)
+            if c > 0:
+                regroup(first_blocks[c])
+            copy_dq(1, c)
+            quantise(first_blocks[c - 1]) if c > 0 else None
+            if c == 2:
+                quantise_dq(1, 0)
+            if c >= 2:
+                transpose_x(c + 2)
+                copy_x(c + 2)
+            if c == 3:
+                quantise_x(4)
+        down_projection(0, 4)
+        quantise_x(5)
+        copy_dq(0, 4)
+        quantise(first_blocks[3])
+        down_projection(0, 5)
+        quantise_dq(1, 1)
+        copy_dq(0, 5)
+
+        def weights_step(keys):
+            steps = []
+            for n, key in enumerate(keys):
+                steps.append(lambda key=key, prev=keys[n - 1] if n else None: (regroup(key), quantise(prev) if prev else None))
+            steps.append(lambda: quantise(keys[-1]))
+            return steps
+
+        def down_step(half, j):
+            def step():
+                down_projection(half, j)
+                copy_dq(half, j)
+                if j % 2 == 1 and half == 1:
+                    quantise_dq(0, j // 2)
+                    quantise_dq(1, j // 2)
+            return step
+
+        def x_steps(j):
+            return [lambda: (transpose_x(j), copy_x(j)), lambda: quantise_x(j)]
+
+        def load_last():
+            load_stage2("up", 1, 1)
+
+        w1 = weights_step([("up", 0, 1), ("up", 1, 1)])
+        w2 = weights_step([("rope", 0, 1), ("rope", 1, 1), ("up", 0, 2), ("up", 1, 2), ("up", 0, 3), ("up", 1, 3)])
+        x6, x7 = x_steps(6), x_steps(7)
+        background = [
+            w1[0], down_step(1, 4), w1[1], down_step(1, 5), w1[2], load_last, x6[0], x6[1], x7[0], x7[1],
+            down_step(0, 6), w2[0], down_step(1, 6), w2[1], down_step(0, 7), w2[2], down_step(1, 7),
+            w2[3], w2[4], w2[5], w2[6],
+        ]
+        units = [(0, 0), (1, 0), (0, 1), (1, 1), (2, 0), (2, 1), (3, 0), (3, 1)]
+        pace = [10, 7, 2, 1, 1, 0, 0, 0]
+
+        def take(n):
+            for step in background[:n]:
+                step()
+            del_n = background[n:]
+            background.clear()
+            background.extend(del_n)
+
+        for n, (group, quad) in enumerate(units):
+            left = pace[n]
+            rotary(group, quad, 0)
+            rotary(group, quad, 1)
+            width = 2 if n in (0, len(units) - 1) else QUAD
+            for jj in range(QUAD):
+                content(group, quad, jj)
+                k = (left + QUAD - 1 - jj) // (QUAD - jj)
+                take(k)
+                left -= k
+                if (jj + 1) % width == 0:
+                    store(group, quad, jj + 1 - width, jj + 1)

@@ -25,7 +25,7 @@ GROUPS = H // GROUP_HEADS
 ROPE_COLS = GROUP_HEADS * DR
 QUAD = 4
 
-VECTOR_COLS = 320
+VECTOR_COLS = 304
 
 FLOPS = 2 * S * D * DQ + 2 * S * DQ * (H * DH + H * DR)
 
@@ -43,7 +43,7 @@ def tile_multiheadlatentattention_pa_kernel(
         name="w2raw", bufs=5
     ) as w2raw, tc.tile_pool(name="wgroup", bufs=3) as wgroup, tc.tile_pool(
         name="agroup", bufs=2
-    ) as agroup, tc.tile_pool(name="xq", bufs=6) as xq, tc.tile_pool(
+    ) as agroup, tc.tile_pool(name="xq", bufs=J) as xq, tc.tile_pool(
         name="wdq", bufs=2 * D_PASSES
     ) as wdq, tc.tile_pool(name="dqq", bufs=J) as dqq, tc.tile_pool(
         name="w2q", bufs=12
@@ -208,21 +208,22 @@ def tile_multiheadlatentattention_pa_kernel(
                     (group % 2) * ROPE_COLS,
                     ROPE_COLS,
                 )
-            shape = [P, 2, GROUP_HEADS, HALF, 2, 2]
-            products = parts.tile(shape, F32, tag="prod", name="products")
-            nc.vector.tensor_tensor(
-                out=products[:],
-                in0=qr[:]
-                .rearrange("p (j h i a) -> p j h i a", j=2, h=GROUP_HEADS, a=2)
-                .unsqueeze(4)
-                .to_broadcast(shape),
-                in1=factor[:, j0 : j0 + 2, :, :, :].unsqueeze(2).to_broadcast(shape),
-                op=MULT,
-            )
+            shape = [P, 2, GROUP_HEADS, HALF, 2]
+            pairs = qr[:].rearrange("p (j h i a) -> p j h i a", j=2, h=GROUP_HEADS, a=2)
+            products = []
+            for a in range(2):
+                product = parts.tile(shape, F32, tag="part%d" % a, name="product")
+                nc.vector.tensor_tensor(
+                    out=product[:],
+                    in0=pairs[:, :, :, :, a : a + 1].to_broadcast(shape),
+                    in1=factor[:, a, j0 : j0 + 2, :, :].unsqueeze(2).to_broadcast(shape),
+                    op=MULT,
+                )
+                products.append(product)
             nc.gpsimd.tensor_tensor(
                 out=result[:, :, 2 * jp : 2 * jp + 2, DH : DH + DR],
-                in0=products[:, :, :, :, :, 0].rearrange("p j h i e -> p h j (i e)"),
-                in1=products[:, :, :, :, :, 1].rearrange("p j h i e -> p h j (i e)"),
+                in0=products[0][:].rearrange("p j h i e -> p h j (i e)"),
+                in1=products[1][:].rearrange("p j h i e -> p h j (i e)"),
                 op=ADD,
             )
 
@@ -242,134 +243,135 @@ def tile_multiheadlatentattention_pa_kernel(
                 in_=results[(group, quad)][:, :, first:last, :],
             )
 
-        load_w_down(0, 0)
         load_x(0)
+        for c in range(D_PASSES):
+            load_w_down(0, c)
+        load_x(1)
+        load_w_down(1, 0)
+        load_x(2)
+        load_w_down(1, 1)
+        load_x(3)
         ident = const.tile([P, P], F32)
         make_identity(nc, ident[:])
         cos_sb = const.tile([P, J, HALF], BF16)
         sin_sb = const.tile([P, J, HALF], BF16)
         nc.scalar.dma_start(out=cos_sb[:], in_=rope_cos.rearrange("(p j) i -> p j i", j=J))
         nc.scalar.dma_start(out=sin_sb[:], in_=rope_sin.rearrange("(p j) i -> p j i", j=J))
-        factor = const.tile([P, J, HALF, 2, 2], F32)
-        nc.gpsimd.tensor_copy(out=factor[:, :, :, 0, 0], in_=cos_sb[:])
-        nc.gpsimd.tensor_copy(out=factor[:, :, :, 1, 0], in_=sin_sb[:])
+        factor = const.tile([P, 2, J, HALF, 2], F32)
+        nc.gpsimd.tensor_copy(out=factor[:, 0, :, :, 0], in_=cos_sb[:])
+        nc.gpsimd.tensor_copy(out=factor[:, 0, :, :, 1], in_=sin_sb[:])
         nc.gpsimd.tensor_scalar(
-            out=factor[:, :, :, 0, 1], in0=sin_sb[:], scalar1=-1.0, scalar2=0.0, op0=MULT, op1=ADD
+            out=factor[:, 1, :, :, 0], in0=sin_sb[:], scalar1=-1.0, scalar2=0.0, op0=MULT, op1=ADD
         )
-        nc.gpsimd.tensor_copy(out=factor[:, :, :, 1, 1], in_=cos_sb[:])
+        nc.gpsimd.tensor_copy(out=factor[:, 1, :, :, 1], in_=cos_sb[:])
 
-        for c in range(1, D_PASSES):
-            load_w_down(0, c)
-            load_x(c)
-        for c in range(2):
-            load_w_down(1, c)
+        blocks = [("down", c, half) for half in range(2) for c in range(D_PASSES)]
+        for name, part in (("up", 0), ("rope", 0), ("up", 1), ("rope", 1), ("up", 2), ("up", 3)):
+            blocks += [(name, g, part) for g in range(DQ_PASSES)]
+        regrouped = []
 
-        for c in range(D_PASSES):
-            transpose_x(c)
-            regroup(("down", c, 0))
-            copy_x(c)
-            if c > 0:
-                quantise(("down", c - 1, 0))
-                quantise_x(c - 1)
-        for c in range(2, D_PASSES):
-            load_w_down(1, c)
-        load_stage2("up", 0, 0)
-        load_stage2("up", 1, 0)
+        def regroup_next():
+            if blocks:
+                regrouped.append(blocks.pop(0))
+                regroup(regrouped[-1])
+
+        def quantise_next():
+            if regrouped:
+                quantise(regrouped.pop(0))
+
+        def down(half, j):
+            down_projection(half, j)
+            copy_dq(half, j)
+
+        def transposed(j):
+            transpose_x(j)
+            copy_x(j)
+
+        regroup_next()
+        transposed(0)
+        regroup_next()
+        quantise_next()
+        quantise_x(0)
+        for n in range(2):
+            regroup_next()
+            quantise_next()
+        quantise_next()
+        load_w_down(1, 2)
         load_x(4)
+        load_w_down(1, 3)
+
+        transposed(1)
         load_x(5)
+        regroup_next()
+        quantise_x(1)
+        quantise_next()
+        load_stage2("up", 0, 0)
+        for j in range(2, QUAD):
+            transposed(j)
+            load_x(j + 4)
+            down(0, j - 2)
+            regroup_next()
+            quantise_x(j)
+            quantise_next()
+        load_stage2("up", 1, 0)
         load_stage2("rope", 0, 0)
         load_stage2("rope", 1, 0)
-        load_x(6)
-        load_x(7)
         load_stage2("up", 0, 1)
+        down(0, 2)
+        regroup_next()
+        quantise_dq(0, 0)
+        quantise_next()
+        down(0, 3)
 
-        regroup(("down", 0, 1))
-        quantise(("down", D_PASSES - 1, 0))
-        quantise_x(D_PASSES - 1)
-        for c in range(D_PASSES):
-            down_projection(0, c)
-            if c > 0:
-                regroup(("down", c, 1))
-            copy_dq(0, c)
-            if c > 0:
-                quantise(("down", c - 1, 1))
-            if c == 2:
-                quantise_dq(0, 0)
+        for pair, half in ((2, 1), (3, 0)):
+            j = 2 * pair
+            transpose_x(j)
+            copy_x(j)
+            transpose_x(j + 1)
+            copy_x(j + 1)
+            regroup_next()
+            quantise_x(j)
+            quantise_next()
+            quantise_x(j + 1)
+            quantise_dq(*((0, 1) if half == 1 else (1, 0)))
+            for jj in (0, 1) if half == 1 else (4, 5):
+                down(half, jj)
+        regroup_next()
+        quantise_next()
+        regroup_next()
+        quantise_dq(0, 2)
+        for half, pair, dq in ((1, 1, (1, 1)), (0, 3, (0, 3))):
+            down(half, 2 * pair)
+            down(half, 2 * pair + 1)
+            regroup_next()
+            quantise_next()
+            if half == 1:
+                quantise_next()
+            quantise_dq(*dq)
 
-        first_blocks = [("up", 0, 0), ("up", 1, 0), ("rope", 0, 0), ("rope", 1, 0)]
-        regroup(first_blocks[0])
-        quantise(("down", D_PASSES - 1, 1))
-        quantise_dq(0, 1)
-        for c in range(4):
-            down_projection(1, c)
-            if c > 0:
-                regroup(first_blocks[c])
-            copy_dq(1, c)
-            quantise(first_blocks[c - 1]) if c > 0 else None
-            if c == 2:
-                quantise_dq(1, 0)
-            if c >= 2:
-                transpose_x(c + 2)
-                copy_x(c + 2)
-            if c == 3:
-                quantise_x(4)
-        down_projection(0, 4)
-        quantise_x(5)
-        copy_dq(0, 4)
-        quantise(first_blocks[3])
-        down_projection(0, 5)
-        quantise_dq(1, 1)
-        copy_dq(0, 5)
-
-        def weights_step(keys):
-            steps = []
-            for n, key in enumerate(keys):
-                steps.append(lambda key=key, prev=keys[n - 1] if n else None: (regroup(key), quantise(prev) if prev else None))
-            steps.append(lambda: quantise(keys[-1]))
-            return steps
-
-        def down_step(half, j):
-            def step():
-                down_projection(half, j)
-                copy_dq(half, j)
-                if j % 2 == 1 and half == 1:
-                    quantise_dq(0, j // 2)
-                    quantise_dq(1, j // 2)
-            return step
-
-        def x_steps(j):
-            return [lambda: (transpose_x(j), copy_x(j)), lambda: quantise_x(j)]
-
-        def load_last():
-            load_stage2("up", 1, 1)
-
-        w1 = weights_step([("up", 0, 1), ("up", 1, 1)])
-        w2 = weights_step([("rope", 0, 1), ("rope", 1, 1), ("up", 0, 2), ("up", 1, 2), ("up", 0, 3), ("up", 1, 3)])
-        x6, x7 = x_steps(6), x_steps(7)
-        background = [
-            w1[0], down_step(1, 4), w1[1], down_step(1, 5), w1[2], load_last, x6[0], x6[1], x7[0], x7[1],
-            down_step(0, 6), w2[0], down_step(1, 6), w2[1], down_step(0, 7), w2[2], down_step(1, 7),
-            w2[3], w2[4], w2[5], w2[6],
-        ]
-        units = [(0, 0), (1, 0), (0, 1), (1, 1), (2, 0), (2, 1), (3, 0), (3, 1)]
-        pace = [10, 7, 2, 1, 1, 0, 0, 0]
-
-        def take(n):
-            for step in background[:n]:
-                step()
-            del_n = background[n:]
-            background.clear()
-            background.extend(del_n)
-
+        load_stage2("up", 1, 1)
+        units = [(group, quad) for group in range(GROUPS) for quad in range(J // QUAD)]
+        down(1, 4)
+        rotary(0, 0, 0)
+        down(1, 5)
+        rotary(0, 0, 1)
+        regroup_next()
+        quantise_next()
+        quantise_dq(1, 2)
+        down(1, 6)
+        down(1, 7)
+        quantise_next()
+        quantise_dq(1, 3)
         for n, (group, quad) in enumerate(units):
-            left = pace[n]
-            rotary(group, quad, 0)
-            rotary(group, quad, 1)
             width = 2 if n in (0, len(units) - 1) else QUAD
             for jj in range(QUAD):
                 content(group, quad, jj)
-                k = (left + QUAD - 1 - jj) // (QUAD - jj)
-                take(k)
-                left -= k
+                if n > 0:
+                    if jj == 0:
+                        regroup_next()
+                    if jj == 2:
+                        quantise_next()
+                if jj % 2 == 1 and n + 1 < len(units):
+                    rotary(units[n + 1][0], units[n + 1][1], jj // 2)
                 if (jj + 1) % width == 0:
                     store(group, quad, jj + 1 - width, jj + 1)

@@ -49,7 +49,7 @@ def tile_multiheadlatentattention_pa_kernel(
         name="w2q", bufs=12
     ) as w2q, tc.tile_pool(name="parts", bufs=2) as parts, tc.tile_pool(
         name="outs", bufs=3
-    ) as outs, tc.psum_pool(name="psum", bufs=8) as psum, tc.manual_schedule():
+    ) as outs, tc.psum_pool(name="psum", bufs=8) as psum:
         x_raw, wd_raw, w2_raw = {}, {}, {}
         x_grouped, x_codes = {}, {}
         grouped_blocks, w_codes = {}, {}

@@ -325,17 +325,16 @@ def tile_multiheadlatentattention_pa_kernel(
 
         for pair, half in ((2, 1), (3, 0)):
             j = 2 * pair
-            transpose_x(j)
-            copy_x(j)
-            transpose_x(j + 1)
-            copy_x(j + 1)
+            first, second = (0, 1) if half == 1 else (4, 5)
+            transposed(j)
             regroup_next()
             quantise_x(j)
+            down(half, first)
+            transposed(j + 1)
             quantise_next()
             quantise_x(j + 1)
             quantise_dq(*((0, 1) if half == 1 else (1, 0)))
-            for jj in (0, 1) if half == 1 else (4, 5):
-                down(half, jj)
+            down(half, second)
         regroup_next()
         quantise_next()
         regroup_next()

@@ -88,12 +88,12 @@ def tile_multiheadlatentattention_pa_kernel(
                 raw = w2_raw[(name, g, part // 2 if name == "up" else 0)]
                 rows = raw[:, :, (part % 2) * BANK : (part % 2 + 1) * BANK]
             grouped = wgroup.tile([P, BANK, PACK], BF16, align_bytes=64, tag="wg", name="grouped")
-            cols = "(i c)" if name == "down" else "(c i)"
-            dst = grouped[:].rearrange("p %s t -> p c t i" % cols, i=4)
-            src = rows.rearrange("p t (c i) -> p c t i", i=4)
-            v = VECTOR_COLS // 4
+            cols, run = ("(i c)", PACK) if name == "down" else ("(c i)", 2 * PACK)
+            dst = grouped[:].rearrange("p %s t -> p c t i" % cols, i=run)
+            src = rows.rearrange("p t (c i) -> p c t i", i=run)
+            v = VECTOR_COLS // run
             nc.vector.tensor_copy(out=dst[:, 0:v, :, :], in_=src[:, 0:v, :, :])
-            nc.scalar.copy(out=dst[:, v : BANK // 4, :, :], in_=src[:, v : BANK // 4, :, :])
+            nc.scalar.copy(out=dst[:, v : BANK // run, :, :], in_=src[:, v : BANK // run, :, :])
             grouped_blocks[key] = grouped
 
         def quantise(key):

@@ -244,13 +244,15 @@ def tile_multiheadlatentattention_pa_kernel(
             )
 
         load_x(0)
-        for c in range(D_PASSES):
-            load_w_down(0, c)
+        load_w_down(0, 0)
+        load_w_down(0, 1)
         load_x(1)
-        load_w_down(1, 0)
+        load_w_down(0, 2)
+        load_w_down(0, 3)
         load_x(2)
-        load_w_down(1, 1)
+        load_w_down(1, 0)
         load_x(3)
+        load_w_down(1, 1)
         ident = const.tile([P, P], F32)
         make_identity(nc, ident[:])
         cos_sb = const.tile([P, J, HALF], BF16)

from concourse import mybir
from concourse.masks import make_identity

BF16 = mybir.dt.bfloat16
F32 = mybir.dt.float32
U32 = mybir.dt.uint32
U8 = mybir.dt.uint8
FP8X4 = mybir.dt.float8_e4m3fn_x4
MULT = mybir.AluOpType.mult
ADD = mybir.AluOpType.add

P = 128
PACK = 4
K_PASS = P * PACK
BANK = 512

S, D, DQ = 1024, 2048, 1024
H, DH, DR = 16, 128, 64
HALF = DR // 2
J = S // P
D_PASSES = D // K_PASS
DQ_PASSES = DQ // K_PASS
GROUP_HEADS = BANK // DH
GROUPS = H // GROUP_HEADS
ROPE_COLS = GROUP_HEADS * DR
QUAD = 4

VECTOR_COLS = 304

FLOPS = 2 * S * D * DQ + 2 * S * DQ * (H * DH + H * DR)


def tile_multiheadlatentattention_pa_kernel(
    tc, x, w_down, w_up, w_rope, rope_cos, rope_sin, out
):
    nc = tc.nc
    x_rows = x.flatten_outer_dims().rearrange("(p j) d -> p j d", j=J)
    out_rows = out.flatten_outer_dims().rearrange("(h p j) f -> p h j f", h=H, j=J)

    with tc.tile_pool(name="const", bufs=1) as const, tc.tile_pool(
        name="xraw", bufs=4
    ) as xraw, tc.tile_pool(name="wdraw", bufs=6) as wdraw, tc.tile_pool(
        name="w2raw", bufs=5
    ) as w2raw, tc.tile_pool(name="wgroup", bufs=3) as wgroup, tc.tile_pool(
        name="agroup", bufs=2
    ) as agroup, tc.tile_pool(name="xq", bufs=J) as xq, tc.tile_pool(
        name="wdq", bufs=2 * D_PASSES
    ) as wdq, tc.tile_pool(name="dqq", bufs=J) as dqq, tc.tile_pool(
        name="w2q", bufs=12
    ) as w2q, tc.tile_pool(name="parts", bufs=2) as parts, tc.tile_pool(
        name="outs", bufs=3
    ) as outs, tc.psum_pool(name="psum", bufs=8) as psum:
        x_raw, wd_raw, w2_raw = {}, {}, {}
        x_grouped, x_codes = {}, {}
        grouped_blocks, w_codes = {}, {}
        dq_acc, dq_grouped, dq_codes = {}, {}, {}
        xt_banks = {}
        results = {}

        def load_x(j):
            t = xraw.tile([P, D], BF16, tag="x", name="x_raw")
            nc.sync.dma_start(out=t[:], in_=x_rows[:, j, :])
            x_raw[j] = t

        def load_w_down(half, c):
            t = wdraw.tile([P, PACK, BANK], BF16, tag="wd", name="wd_raw")
            nc.sync.dma_start(
                out=t[:],
                in_=w_down[c * K_PASS : (c + 1) * K_PASS, half * BANK : (half + 1) * BANK].rearrange(
                    "(p t) n -> p t n", t=PACK
                ),
            )
            wd_raw[("down", c, half)] = t

        def load_stage2(name, g, half):
            src = w_up[:, half * 2 * BANK : (half + 1) * 2 * BANK] if name == "up" else w_rope
            t = w2raw.tile([P, PACK, 2 * BANK], BF16, tag="w2", name="w2_raw")
            nc.sync.dma_start(
                out=t[:], in_=src[g * K_PASS : (g + 1) * K_PASS, :].rearrange("(p t) n -> p t n", t=PACK)
            )
            w2_raw[(name, g, half)] = t

        def regroup(key):
            name, g, part = key
            if name == "down":
                rows = wd_raw[key][:]
            else:
                raw = w2_raw[(name, g, part // 2 if name == "up" else 0)]
                rows = raw[:, :, (part % 2) * BANK : (part % 2 + 1) * BANK]
            grouped = wgroup.tile([P, BANK, PACK], BF16, align_bytes=64, tag="wg", name="grouped")
            cols, run = ("(i c)", PACK) if name == "down" else ("(c i)", 2 * PACK)
            dst = grouped[:].rearrange("p %s t -> p c t i" % cols, i=run)
            src = rows.rearrange("p t (c i) -> p c t i", i=run)
            v = VECTOR_COLS // run
            nc.vector.tensor_copy(out=dst[:, 0:v, :, :], in_=src[:, 0:v, :, :])
            nc.scalar.copy(out=dst[:, v : BANK // run, :, :], in_=src[:, v : BANK // run, :, :])
            grouped_blocks[key] = grouped

        def quantise(key):
            pool = wdq if key[0] == "down" else w2q
            codes = pool.tile([P, BANK], U32, align_bytes=64, tag="codes", name="w_codes")
            scales = pool.tile([P, BANK], U8, align_bytes=64, tag="scales", name="w_scales")
            nc.vector.quantize_mx(
                out=codes[:].bitcast(FP8X4),
                scales=scales[:],
                in_=grouped_blocks[key][:].rearrange("p n t -> p (n t)"),
            )
            w_codes[key] = (codes, scales)

        def transpose_x(j):
            words = x_raw[j][:].bitcast(F32)
            banks = []
            for b in range(2):
                xt = psum.tile([P, BANK], F32, tag="bank", name="xt")
                for cl in range(2):
                    for u in range(2):
                        col0 = (2 * b + cl) * 2 * P
                        nc.tensor.transpose(
                            xt[:, (2 * cl + u) * P : (2 * cl + u + 1) * P],
                            words[:, col0 + u : col0 + 2 * P : 2],
                            ident[:],
                        )
                banks.append(xt)
            xt_banks[j] = banks

        def copy_x(j):
            grouped = agroup.tile([P, D], BF16, align_bytes=64, tag="xg", name="x_grouped")
            words = grouped[:].bitcast(F32).rearrange("q (c s u) -> q c s u", c=D_PASSES, u=2)
            for b in range(2):
                nc.scalar.copy(
                    out=words[:, 2 * b : 2 * b + 2, :, :],
                    in_=xt_banks[j][b][:].rearrange("q (c u s) -> q c s u", c=2, u=2),
                )
            x_grouped[j] = grouped

        def quantise_x(j):
            codes = xq.tile([P, D_PASSES * P], U32, align_bytes=64, tag="codes", name="x_codes")
            scales = xq.tile([P, D_PASSES * P], U8, align_bytes=64, tag="scales", name="x_scales")
            nc.vector.quantize_mx(out=codes[:].bitcast(FP8X4), scales=scales[:], in_=x_grouped[j][:])
            x_codes[j] = (codes, scales)

        def down_projection(half, j):
            xc, xs = x_codes[j]
            acc = psum.tile([P, BANK], F32, tag="bank", name="dq_acc")
            for t in range(PACK):
                for c in range(D_PASSES):
                    wc, ws = w_codes[("down", c, half)]
                    nc.tensor.matmul_mx(
                        out=acc[:, t * P : (t + 1) * P],
                        lhsT=wc[:, t * P : (t + 1) * P].bitcast(FP8X4),
                        lhsT_scale=ws[:, t * P : (t + 1) * P],
                        rhs=xc[:, c * P : (c + 1) * P].bitcast(FP8X4),
                        rhs_scale=xs[:, c * P : (c + 1) * P],
                        start=(c == 0),
                        stop=(c == D_PASSES - 1),
                    )
            dq_acc[(half, j)] = acc

        def copy_dq(half, j):
            if j % 2 == 0:
                dq_grouped[(half, j // 2)] = agroup.tile(
                    [P, 2, P, PACK], BF16, align_bytes=64, tag="dqg", name="dq_grouped"
                )
            nc.scalar.copy(
                out=dq_grouped[(half, j // 2)][:, j % 2, :, :],
                in_=dq_acc[(half, j)][:].rearrange("p (t s) -> p s t", t=PACK),
            )

        def quantise_dq(half, pair):
            codes = dqq.tile([P, 2 * P], U32, align_bytes=64, tag="codes", name="dq_codes")
            scales = dqq.tile([P, 2 * P], U8, align_bytes=64, tag="scales", name="dq_scales")
            nc.vector.quantize_mx(
                out=codes[:].bitcast(FP8X4),
                scales=scales[:],
                in_=dq_grouped[(half, pair)][:].rearrange("p j s t -> p (j s t)"),
            )
            dq_codes[(half, pair)] = (codes, scales)

        def up_projection(acc, j, weights, col0, width):
            for g in range(DQ_PASSES):
                ac, asc = dq_codes[(g, j // 2)]
                wc, ws = weights[g]
                tok = slice((j % 2) * P, (j % 2 + 1) * P)
                nc.tensor.matmul_mx(
                    out=acc,
                    lhsT=ac[:, tok].bitcast(FP8X4),
                    lhsT_scale=asc[:, tok],
                    rhs=wc[:, col0 : col0 + width].bitcast(FP8X4),
                    rhs_scale=ws[:, col0 : col0 + width],
                    start=(g == 0),
                    stop=(g == DQ_PASSES - 1),
                )

        def rotary(group, quad, jp):
            if jp == 0:
                results[(group, quad)] = outs.tile(
                    [P, GROUP_HEADS, QUAD, DH + DR], F32, tag="res", name="result"
                )
            result = results[(group, quad)]
            rope_w = [w_codes[("rope", g, group // 2)] for g in range(DQ_PASSES)]
            j0 = quad * QUAD + 2 * jp
            qr = psum.tile([P, BANK], F32, tag="bank", name="qr")
            for jl in range(2):
                up_projection(
                    qr[:, jl * ROPE_COLS : (jl + 1) * ROPE_COLS],
                    j0 + jl,
                    rope_w,
                    (group % 2) * ROPE_COLS,
                    ROPE_COLS,
                )
            shape = [P, 2, GROUP_HEADS, HALF, 2]
            pairs = qr[:].rearrange("p (j h i a) -> p j h i a", j=2, h=GROUP_HEADS, a=2)
            products = []
            for a in range(2):
                product = parts.tile(shape, F32, tag="part%d" % a, name="product")
                nc.vector.tensor_tensor(
                    out=product[:],
                    in0=pairs[:, :, :, :, a : a + 1].to_broadcast(shape),
                    in1=factor[:, a, j0 : j0 + 2, :, :].unsqueeze(2).to_broadcast(shape),
                    op=MULT,
                )
                products.append(product)
            nc.gpsimd.tensor_tensor(
                out=result[:, :, 2 * jp : 2 * jp + 2, DH : DH + DR],
                in0=products[0][:].rearrange("p j h i e -> p h j (i e)"),
                in1=products[1][:].rearrange("p j h i e -> p h j (i e)"),
                op=ADD,
            )

        def content(group, quad, jj):
            up_w = [w_codes[("up", g, group)] for g in range(DQ_PASSES)]
            qc = psum.tile([P, BANK], F32, tag="bank", name="qc")
            up_projection(qc[:], quad * QUAD + jj, up_w, 0, BANK)
            nc.scalar.copy(
                out=results[(group, quad)][:, :, jj, 0:DH],
                in_=qc[:].rearrange("p (h d) -> p h d", h=GROUP_HEADS),
            )

        def store(group, quad, first, last):
            heads = slice(group * GROUP_HEADS, (group + 1) * GROUP_HEADS)
            nc.sync.dma_start(
                out=out_rows[:, heads, quad * QUAD + first : quad * QUAD + last, :],
                in_=results[(group, quad)][:, :, first:last, :],
            )

        load_x(0)
        load_w_down(0, 0)
        load_w_down(0, 1)
        load_x(1)
        load_w_down(0, 2)
        load_w_down(0, 3)
        load_x(2)
        load_w_down(1, 0)
        load_x(3)
        load_w_down(1, 1)
        ident = const.tile([P, P], F32)
        make_identity(nc, ident[:])
        cos_sb = const.tile([P, J, HALF], BF16)
        sin_sb = const.tile([P, J, HALF], BF16)
        nc.scalar.dma_start(out=cos_sb[:], in_=rope_cos.rearrange("(p j) i -> p j i", j=J))
        nc.scalar.dma_start(out=sin_sb[:], in_=rope_sin.rearrange("(p j) i -> p j i", j=J))
        factor = const.tile([P, 2, J, HALF, 2], F32)
        nc.gpsimd.tensor_copy(out=factor[:, 0, :, :, 0], in_=cos_sb[:])
        nc.gpsimd.tensor_copy(out=factor[:, 0, :, :, 1], in_=sin_sb[:])
        nc.gpsimd.tensor_scalar(
            out=factor[:, 1, :, :, 0], in0=sin_sb[:], scalar1=-1.0, scalar2=0.0, op0=MULT, op1=ADD
        )
        nc.gpsimd.tensor_copy(out=factor[:, 1, :, :, 1], in_=cos_sb[:])

        blocks = [("down", c, half) for half in range(2) for c in range(D_PASSES)]
        for name, part in (("up", 0), ("rope", 0), ("up", 1), ("rope", 1), ("up", 2), ("up", 3)):
            blocks += [(name, g, part) for g in range(DQ_PASSES)]
        regrouped = []

        def regroup_next():
            if blocks:
                regrouped.append(blocks.pop(0))
                regroup(regrouped[-1])

        def quantise_next():
            if regrouped:
                quantise(regrouped.pop(0))

        def down(half, j):
            down_projection(half, j)
            copy_dq(half, j)

        def transposed(j):
            transpose_x(j)
            copy_x(j)

        regroup_next()
        transposed(0)
        regroup_next()
        quantise_next()
        quantise_x(0)
        for n in range(2):
            regroup_next()
            quantise_next()
        quantise_next()
        load_w_down(1, 2)
        load_x(4)
        load_w_down(1, 3)

        transposed(1)
        load_x(5)
        regroup_next()
        quantise_x(1)
        quantise_next()
        load_stage2("up", 0, 0)
        for j in range(2, QUAD):
            transposed(j)
            load_x(j + 4)
            down(0, j - 2)
            regroup_next()
            quantise_x(j)
            quantise_next()
        load_stage2("up", 1, 0)
        load_stage2("rope", 0, 0)
        load_stage2("rope", 1, 0)
        load_stage2("up", 0, 1)
        down(0, 2)
        regroup_next()
        quantise_dq(0, 0)
        quantise_next()
        down(0, 3)

        for pair, half in ((2, 1), (3, 0)):
            j = 2 * pair
            first, second = (0, 1) if half == 1 else (4, 5)
            transposed(j)
            regroup_next()
            quantise_x(j)
            down(half, first)
            transposed(j + 1)
            quantise_next()
            quantise_x(j + 1)
            quantise_dq(*((0, 1) if half == 1 else (1, 0)))
            down(half, second)
        regroup_next()
        quantise_next()
        regroup_next()
        quantise_dq(0, 2)
        for half, pair, dq in ((1, 1, (1, 1)), (0, 3, (0, 3))):
            down(half, 2 * pair)
            down(half, 2 * pair + 1)
            regroup_next()
            quantise_next()
            if half == 1:
                quantise_next()
            quantise_dq(*dq)

        load_stage2("up", 1, 1)
        units = [(group, quad) for group in range(GROUPS) for quad in range(J // QUAD)]
        down(1, 4)
        rotary(0, 0, 0)
        down(1, 5)
        rotary(0, 0, 1)
        regroup_next()
        quantise_next()
        quantise_dq(1, 2)
        down(1, 6)
        down(1, 7)
        quantise_next()
        quantise_dq(1, 3)
        for n, (group, quad) in enumerate(units):
            width = 2 if n in (0, len(units) - 1) else QUAD
            for jj in range(QUAD):
                content(group, quad, jj)
                if n > 0:
                    if jj == 0:
                        regroup_next()
                    if jj == 2:
                        quantise_next()
                if jj % 2 == 1 and n + 1 < len(units):
                    rotary(units[n + 1][0], units[n + 1][1], jj // 2)
                if (jj + 1) % width == 0:
                    store(group, quad, jj + 1 - width, jj + 1)
